import numpy as np
import ml_dtypes


def mxq(x, axis, fmt="e4m3"):
    dtype, down = {"e4m3": (ml_dtypes.float8_e4m3fn, 7), "e5m2": (ml_dtypes.float8_e5m2, 14)}[fmt]
    v = np.moveaxis(np.asarray(x, np.float32).astype(ml_dtypes.bfloat16).astype(np.float64), axis, -1)
    blocks = v.reshape(v.shape[:-1] + (-1, 32))
    amax = np.abs(blocks).max(-1, keepdims=True)
    byte = np.maximum(np.where(amax > 0, np.frexp(amax)[1] - 1 + 127, 0) - down, 1)
    scale = np.exp2(byte - 127.0)
    codes = (blocks / scale).astype(np.float32).astype(dtype).astype(np.float64)
    return np.moveaxis((codes * scale).reshape(v.shape), -1, axis)


WIDE = False


def mx_kscale(k):
    if not WIDE:
        return np.ones(k)
    levels = np.array([10, -10, 5, -5, 0])
    a = np.random.permutation(np.resize(levels, k // 512 * 4)).reshape(k // 512, 4)
    idx = np.arange(k)
    return np.exp2(a[idx // 512, idx % 128 // 32])


BF16 = ml_dtypes.bfloat16


def bf(x):
    return np.asarray(x, np.float32).astype(BF16)


def f64(x):
    return np.asarray(x).astype(np.float64)


B, S, H, NH, QB = 4, 1024, 512, 4, 512
D = H // NH
MASKED = -10000.0


def alibi_slopes():
    base = 2.0 ** (-(2.0 ** -(np.log2(NH) - 3.0)))
    return base ** np.arange(1, 1 + NH)


def setup_inputs():
    s = mx_kscale(H)
    return {"q": bf(np.random.standard_normal((B, S, NH, D))),
            "k": bf(np.random.standard_normal((B, S, NH, D))),
            "hidden_states": bf(np.random.standard_normal((B, S, H)) * s),
            "w_v": bf(np.random.standard_normal((H, H)) / np.sqrt(H) / s[None, :]),
            "b_v": bf(np.random.standard_normal(H) * 0.2)}


def reference(q, k, hidden_states, w_v, b_v):
    qt = f64(q).transpose(0, 2, 1, 3)
    kt = f64(k).transpose(0, 2, 3, 1)
    v = (mxq(f64(hidden_states), 2, "e4m3") @ mxq(f64(w_v), 1, "e4m3").T) + f64(b_v)
    vq = mxq(v.reshape(B, S, NH, D).transpose(0, 2, 1, 3), 2, "e4m3")
    slopes = alibi_slopes()
    pos = np.arange(S)
    blocks = []
    for q0 in range(0, S, QB):
        n = q0 + QB
        s = qt[:, :, q0:n] @ kt[:, :, :, :n] / np.sqrt(D) + slopes[None, :, None, None] * pos[None, None, None, :n]
        causal = pos[None, :n] <= pos[q0:n, None]
        s = np.where(causal, s, MASKED)
        e = np.exp(s - s.max(-1, keepdims=True)) * causal
        blocks.append((mxq(e, 3, "e4m3") @ vq[:, :, :n]) / e.sum(-1, keepdims=True))
    return np.concatenate(blocks, axis=2).transpose(0, 2, 1, 3).reshape(B, S, H)

@@ -1,0 +1,400 @@
+import math
+from contextlib import ExitStack
+
+import concourse.mybir as mybir
+from concourse.masks import make_identity
+
+BF16 = mybir.dt.bfloat16
+F32 = mybir.dt.float32
+I32 = mybir.dt.int32
+U32 = mybir.dt.uint32
+U8 = mybir.dt.uint8
+FP8X4 = mybir.dt.float8_e4m3fn_x4
+ALU = mybir.AluOpType
+ACT = mybir.ActivationFunctionType
+AX = mybir.AxisListType
+
+B, S, H, NH = 4, 1024, 512, 4
+D = H // NH
+P = 128
+NT = S // P
+BANK = 512
+K_PASS = 512
+SCALE = 1.0 / math.sqrt(D)
+MASKED = -131072.0
+
+FLOPS = 2 * B * S * H * H + 2 * (2 * B * NH * D * (512 * 512 + 512 * 1024))
+
+
+def tile_bloomattention_pa_t_kernel(tc, q, k, hidden_states, w_v, b_v, out):
+    nc = tc.nc
+    with ExitStack() as ctx:
+        ctx.enter_context(tc.manual_schedule())
+        const = ctx.enter_context(tc.tile_pool(name="const", bufs=1))
+        raw = ctx.enter_context(tc.tile_pool(name="raw", bufs=2))
+        batch = ctx.enter_context(tc.tile_pool(name="batch", bufs=2))
+        stage = ctx.enter_context(tc.tile_pool(name="stage", bufs=1))
+        flow = ctx.enter_context(tc.tile_pool(name="flow", bufs=2))
+        small = ctx.enter_context(tc.tile_pool(name="small", bufs=4))
+        wide_psum = ctx.enter_context(tc.psum_pool(name="wide_psum", bufs=4))
+        turn_psum = ctx.enter_context(tc.psum_pool(name="turn_psum", bufs=2))
+        mx_psum = ctx.enter_context(tc.psum_pool(name="mx_psum", bufs=2))
+
+        loaded = {}
+
+        def load(b):
+            hid_raw = raw.tile([P, 8 * H], BF16)
+            k_raw = raw.tile([P, NT * H], BF16)
+            q_raw = raw.tile([P, NT * H], BF16)
+            nc.sync.dma_start(
+                out=hid_raw[:].rearrange("p (a x) -> p a x", a=4),
+                in_=hidden_states[b].rearrange("(a p e) f -> p a (e f)", p=P, e=2),
+            )
+            nc.sync.dma_start(
+                out=k_raw[:].rearrange("p (t x) -> p t x", t=NT),
+                in_=k[b].rearrange("(t p) h d -> p t (h d)", p=P),
+            )
+            nc.sync.dma_start(
+                out=q_raw[:].rearrange("p (t x) -> p t x", t=NT),
+                in_=q[b].rearrange("(t p) h d -> p t (h d)", p=P),
+            )
+            loaded[b] = {"hid": hid_raw, "k": k_raw, "q": q_raw}
+
+        w_raw = const.tile([P, NH * H], BF16)
+        nc.sync.dma_start(
+            out=w_raw[:].rearrange("p (r f) -> p r f", r=NH),
+            in_=w_v.rearrange("(r p) f -> p r f", p=P),
+        )
+        load(0)
+        bias_bc = const.tile([P, H], BF16)
+        nc.sync.dma_start(out=bias_bc[:], in_=b_v.partition_broadcast(P))
+        load(1)
+
+        ident_f32 = const.tile([P, P], F32)
+        make_identity(nc, ident_f32[:])
+        ident_bf = const.tile([P, P], BF16)
+        make_identity(nc, ident_bf[:])
+
+        steps = const.tile([P, NT], I32)
+        nc.gpsimd.iota(steps[:], pattern=[[-P, NT]], base=1 - P, channel_multiplier=1)
+        after = const.tile([P, P], F32)
+        nc.gpsimd.memset(after[:], 0.0)
+        nc.gpsimd.affine_select(
+            out=after[:],
+            in_=after[:],
+            compare_op=ALU.is_ge,
+            fill=MASKED,
+            base=0,
+            pattern=[[1, P]],
+            channel_multiplier=-1,
+        )
+        slope_col = const.tile([P, NH, NT], F32)
+        diag_bias = {}
+        for h in range(NH):
+            slope = 0.25 ** (h + 1)
+            nc.vector.tensor_scalar(
+                out=slope_col[:, h, :], in0=steps[:], scalar1=slope / SCALE, scalar2=None, op0=ALU.mult
+            )
+            diag_bias[h] = const.tile([P, P], F32, name="diag_bias%d" % h)
+            nc.vector.tensor_scalar(
+                out=diag_bias[h][:], in0=after[:], scalar1=slope_col[:, h, 0:1], scalar2=None, op0=ALU.add
+            )
+
+        e_tiles = {}
+        for t in range(NT):
+            width = K_PASS * (t // 4 + 1)
+            for parity in range(2):
+                e_tile = const.tile([P, width], BF16, name="e_%d_%d" % (t, parity))
+                if (t + 1) * P < width:
+                    nc.gpsimd.memset(e_tile[:, (t + 1) * P :], 0.0)
+                e_tiles[(t, parity)] = e_tile
+
+        def empty_bank(index, dst, src):
+            if index % 2 == 0:
+                nc.scalar.copy(out=dst, in_=src)
+            else:
+                nc.vector.tensor_copy(out=dst, in_=src)
+
+        def turn_words(raw_words, grouped_words, pair):
+            bank = wide_psum.tile([P, 2, 2, P], F32, tag="wide")
+            for s in range(2):
+                for u in range(2):
+                    first = ((2 * pair + s) * 2 + u) * P
+                    nc.tensor.transpose(bank[:, s, u, :], raw_words[:, first : first + P], ident_f32[:])
+            return (
+                pair,
+                grouped_words[:, pair * BANK : (pair + 1) * BANK].rearrange("p (s r u) -> p s r u", s=2, u=2),
+                bank[:].rearrange("p s u r -> p s r u"),
+            )
+
+        def turn_head(src, dst, h):
+            bank = wide_psum.tile([P, NT, P], BF16, tag="wide")
+            for t in range(NT):
+                first = t * H + h * D
+                nc.tensor.transpose(bank[:, t, :], src[:, first : first + D], ident_bf[:])
+            return (h, dst[:, h, :], bank[:].rearrange("p t r -> p (t r)"))
+
+        w_grouped = const.tile([P, NH * H], BF16, align_bytes=64)
+        w_codes = const.tile([P, H], U32, align_bytes=64)
+        w_scales = const.tile([P, H], U8, align_bytes=64)
+        for pair in range(NH // 2):
+            empty_bank(*turn_words(w_raw[:].bitcast(F32), w_grouped[:].bitcast(F32), pair))
+        nc.vector.quantize_mx(out=w_codes[:].bitcast(FP8X4), scales=w_scales[:], in_=w_grouped[:])
+
+        ready = {}
+
+        def turn_hidden(b, pair):
+            if pair == 0:
+                hid_grouped = stage.tile([P, 8 * H], BF16, align_bytes=64)
+                ready[b] = {"hid_grouped": hid_grouped}
+            return turn_words(loaded[b]["hid"][:].bitcast(F32), ready[b]["hid_grouped"][:].bitcast(F32), pair)
+
+        def turn_keys(b, h):
+            if h == 0:
+                kT = batch.tile([P, NH, S], BF16)
+                ready[b]["kT"] = kT
+            return turn_head(loaded[b]["k"], ready[b]["kT"], h)
+
+        def turn_queries(b, h):
+            if h == 0:
+                qT = batch.tile([P, NH, S], BF16)
+                ready[b]["qT"] = qT
+            return turn_head(loaded[b]["q"], ready[b]["qT"], h)
+
+        def quantise_hidden(b):
+            hid_codes = stage.tile([P, 8 * P], U32, align_bytes=64)
+            hid_scales = stage.tile([P, 8 * P], U8, align_bytes=64)
+            ready[b]["hid_codes"] = hid_codes
+            ready[b]["hid_scales"] = hid_scales
+            nc.vector.quantize_mx(
+                out=ready[b]["hid_codes"][:].bitcast(FP8X4),
+                scales=ready[b]["hid_scales"][:],
+                in_=ready[b]["hid_grouped"][:],
+            )
+
+        def project_values(b, g, h):
+            acc = mx_psum.tile([P, 4, D], F32, tag="mx")
+            cols = slice(h * D, (h + 1) * D)
+            for j in range(4):
+                rows = slice((4 * g + j) * P, (4 * g + j + 1) * P)
+                nc.tensor.matmul_mx(
+                    out=acc[:, j, :],
+                    lhsT=ready[b]["hid_codes"][:, rows].bitcast(FP8X4),
+                    lhsT_scale=ready[b]["hid_scales"][:, rows],
+                    rhs=w_codes[:, cols].bitcast(FP8X4),
+                    rhs_scale=w_scales[:, cols],
+                    start=True,
+                    stop=True,
+                )
+            ready[b]["acc"] = acc
+
+        def add_bias(b, g, h):
+            if h == 0:
+                v_grouped = flow.tile([P, NH, D, 4], BF16, align_bytes=64)
+                ready[b]["v_grouped"] = v_grouped
+            nc.vector.tensor_tensor(
+                out=ready[b]["v_grouped"][:, h, :, :],
+                in0=ready[b]["acc"][:].rearrange("p j d -> p d j"),
+                in1=bias_bc[:, h * D : (h + 1) * D].unsqueeze(2).to_broadcast([P, D, 4]),
+                op=ALU.add,
+            )
+            if h == NH - 1:
+                if g == 0:
+                    v_codes = batch.tile([P, 2, H], U32, align_bytes=64)
+                    v_scales = batch.tile([P, 2, H], U8, align_bytes=64)
+                    ready[b]["v_codes"] = v_codes
+                    ready[b]["v_scales"] = v_scales
+                nc.vector.quantize_mx(
+                    out=ready[b]["v_codes"][:, g, :].bitcast(FP8X4),
+                    scales=ready[b]["v_scales"][:, g, :],
+                    in_=ready[b]["v_grouped"][:].rearrange("p h d j -> p (h d j)"),
+                )
+
+        units = [(b, t, h) for b in range(B) for t in range(NT) for h in range(NH)]
+        live = {}
+        tile_live = {}
+
+        def key_banks(t):
+            n_keys = (t + 1) * P
+            return [(k0, min(BANK, n_keys - k0)) for k0 in range(0, n_keys, BANK)]
+
+        def scores(n):
+            b, t, h = units[n]
+            banks = []
+            for k0, width in key_banks(t):
+                sc = wide_psum.tile([P, BANK], F32, tag="wide")
+                for c0 in range(0, width, P):
+                    dist = t - (k0 + c0) // P
+                    if dist == 0:
+                        added = diag_bias[h][:]
+                    else:
+                        added = slope_col[:, h, dist : dist + 1].to_broadcast([P, P])
+                    nc.tensor.matmul(
+                        out=sc[:, c0 : c0 + P],
+                        lhsT=added,
+                        rhs=ident_f32[:],
+                        is_transpose=True,
+                        start=(c0 == 0),
+                        stop=False,
+                    )
+                nc.tensor.matmul(
+                    out=sc[:, :width],
+                    lhsT=ready[b]["qT"][:, h, t * P : (t + 1) * P],
+                    rhs=ready[b]["kT"][:, h, k0 : k0 + width],
+                    start=False,
+                    stop=True,
+                )
+                banks.append((sc, k0, width))
+            live[n] = {"banks": banks}
+
+        def row_max(n):
+            banks = live[n]["banks"]
+            tops = small.tile([P, 2], F32)
+            for i, (sc, k0, width) in enumerate(banks):
+                nc.vector.tensor_reduce(out=tops[:, i : i + 1], in_=sc[:, :width], axis=AX.X, op=ALU.max)
+            shift = small.tile([P, 1], F32)
+            if len(banks) == 2:
+                nc.vector.tensor_scalar(
+                    out=shift[:], in0=tops[:, 0:1], scalar1=tops[:, 1:2], scalar2=-SCALE, op0=ALU.max, op1=ALU.mult
+                )
+            else:
+                nc.vector.tensor_scalar(out=shift[:], in0=tops[:, 0:1], scalar1=-SCALE, scalar2=None, op0=ALU.mult)
+            live[n]["shift"] = shift
+
+        def exponentials(n):
+            b, t, h = units[n]
+            if h == 0:
+                part_sums = small.tile([P, NH, 2], F32)
+                tile_live[(b, t)] = {"part_sums": part_sums}
+            part_sums = tile_live[(b, t)]["part_sums"]
+            e_tile = e_tiles[(t, h % 2)]
+            for i, (sc, k0, width) in enumerate(live[n]["banks"]):
+                nc.scalar.activation(
+                    out=e_tile[:, k0 : k0 + width],
+                    in_=sc[:, :width],
+                    func=ACT.Exp,
+                    bias=live[n]["shift"][:, 0:1],
+                    scale=SCALE,
+                    accum_out=part_sums[:, h, i : i + 1],
+                )
+
+        def turn(n):
+            b, t, h = units[n]
+            passes = t // 4 + 1
+            e_words = e_tiles[(t, h % 2)][:].bitcast(F32)
+            turned = turn_psum.tile([P, 2, 2, P], F32, tag="turn")
+            for g in range(passes):
+                for u in range(2):
+                    first = (2 * g + u) * P
+                    nc.tensor.transpose(turned[:, g, u, :], e_words[:, first : first + P], ident_f32[:])
+            live[n]["turned"] = turned
+
+        def regroup(n):
+            b, t, h = units[n]
+            passes = t // 4 + 1
+            e_grouped = flow.tile([P, 2 * K_PASS], BF16, align_bytes=64)
+            nc.scalar.copy(
+                out=e_grouped[:].bitcast(F32)[:, : passes * 2 * P].rearrange("p (g i u) -> p g i u", g=passes, u=2),
+                in_=live[n]["turned"][:, :passes, :, :].rearrange("p g u i -> p g i u"),
+            )
+            live[n]["e_grouped"] = e_grouped
+
+        def quantise(n):
+            b, t, h = units[n]
+            passes = t // 4 + 1
+            if h == 0:
+                e_codes = flow.tile([P, NH, 2 * P], U32, align_bytes=64)
+                e_scales = flow.tile([P, NH, 2 * P], U8, align_bytes=64)
+                tile_live[(b, t)]["e_codes"] = e_codes
+                tile_live[(b, t)]["e_scales"] = e_scales
+            nc.vector.quantize_mx(
+                out=tile_live[(b, t)]["e_codes"][:, h, : passes * P].bitcast(FP8X4),
+                scales=tile_live[(b, t)]["e_scales"][:, h, : passes * P],
+                in_=live[n]["e_grouped"][:, : passes * K_PASS],
+            )
+
+        def weighted_values(b, t):
+            passes = t // 4 + 1
+            e_codes, e_scales = tile_live[(b, t)]["e_codes"], tile_live[(b, t)]["e_scales"]
+            acc = mx_psum.tile([P, NH, D], F32, tag="mx")
+            for h in range(NH):
+                for g in range(passes):
+                    nc.tensor.matmul_mx(
+                        out=acc[:, h, :],
+                        lhsT=e_codes[:, h, g * P : (g + 1) * P].bitcast(FP8X4),
+                        lhsT_scale=e_scales[:, h, g * P : (g + 1) * P],
+                        rhs=ready[b]["v_codes"][:, g, h * D : (h + 1) * D].bitcast(FP8X4),
+                        rhs_scale=ready[b]["v_scales"][:, g, h * D : (h + 1) * D],
+                        start=(g == 0),
+                        stop=(g == passes - 1),
+                    )
+            tile_live[(b, t)]["acc"] = acc
+
+        def normalise_and_store(b, t):
+            passes = t // 4 + 1
+            row_sum = small.tile([P, NH], F32)
+            nc.vector.tensor_reduce(
+                out=row_sum[:], in_=tile_live[(b, t)]["part_sums"][:, :, :passes], axis=AX.X, op=ALU.add
+            )
+            inverse = small.tile([P, NH], F32)
+            nc.vector.reciprocal(inverse[:], row_sum[:])
+            result = flow.tile([P, NH, D], F32)
+            nc.vector.tensor_tensor(
+                out=result[:],
+                in0=tile_live[(b, t)]["acc"][:],
+                in1=inverse[:].unsqueeze(2).to_broadcast([P, NH, D]),
+                op=ALU.mult,
+            )
+            nc.sync.dma_start(out=out[b, t * P : (t + 1) * P, :], in_=result[:].rearrange("p h d -> p (h d)"))
+
+        for pair in range(4):
+            empty_bank(*turn_hidden(0, pair))
+        quantise_hidden(0)
+        for h in range(NH):
+            empty_bank(*turn_keys(0, h))
+        for h in range(NH):
+            empty_bank(*turn_queries(0, h))
+        for g in range(2):
+            for h in range(NH):
+                project_values(0, g, h)
+                add_bias(0, g, h)
+
+        n_units = len(units)
+        for n in range(n_units + 3):
+            closing = n >= 3 and units[n - 3][2] == NH - 1
+            if n >= 3:
+                quantise(n - 3)
+            if 2 <= n < n_units + 2:
+                turn(n - 2)
+            leaving = None
+            if n < n_units:
+                b, t, h = units[n]
+                if b + 2 < B and t == 0 and h == 0:
+                    load(b + 2)
+                if b + 1 < B:
+                    if t == 0:
+                        leaving = turn_hidden(b + 1, h)
+                    if t == 1 and h == 0:
+                        quantise_hidden(b + 1)
+                    if t == 1:
+                        leaving = turn_keys(b + 1, h)
+                    if t == 2:
+                        leaving = turn_queries(b + 1, h)
+                scores(n)
+            if closing:
+                done_b, done_t = units[n - 3][0], units[n - 3][1]
+                weighted_values(done_b, done_t)
+                if done_b + 1 < B:
+                    project_values(done_b + 1, done_t // 4, done_t % 4)
+            if n < n_units:
+                row_max(n)
+            if 1 <= n < n_units + 1:
+                exponentials(n - 1)
+            if 2 <= n < n_units + 2:
+                regroup(n - 2)
+            if closing:
+                normalise_and_store(done_b, done_t)
+                if done_b + 1 < B:
+                    add_bias(done_b + 1, done_t // 4, done_t % 4)
+            if leaving is not None:
+                empty_bank(*leaving)

@@ -29,7 +29,6 @@ FLOPS = 2 * B * S * H * H + 2 * (2 * B * NH * D * (512 * 512 + 512 * 1024))
 def tile_bloomattention_pa_t_kernel(tc, q, k, hidden_states, w_v, b_v, out):
     nc = tc.nc
     with ExitStack() as ctx:
-        ctx.enter_context(tc.manual_schedule())
         const = ctx.enter_context(tc.tile_pool(name="const", bufs=1))
         raw = ctx.enter_context(tc.tile_pool(name="raw", bufs=2))
         batch = ctx.enter_context(tc.tile_pool(name="batch", bufs=2))

@@ -12,7 +12,6 @@ U8 = mybir.dt.uint8
 FP8X4 = mybir.dt.float8_e4m3fn_x4
 ALU = mybir.AluOpType
 ACT = mybir.ActivationFunctionType
-AX = mybir.AxisListType
 
 B, S, H, NH = 4, 1024, 512, 4
 D = H // NH
@@ -35,6 +34,7 @@ def tile_bloomattention_pa_t_kernel(tc, q, k, hidden_states, w_v, b_v, out):
         stage = ctx.enter_context(tc.tile_pool(name="stage", bufs=1))
         flow = ctx.enter_context(tc.tile_pool(name="flow", bufs=2))
         small = ctx.enter_context(tc.tile_pool(name="small", bufs=4))
+        score_pool = ctx.enter_context(tc.tile_pool(name="score_pool", bufs=3))
         wide_psum = ctx.enter_context(tc.psum_pool(name="wide_psum", bufs=4))
         turn_psum = ctx.enter_context(tc.psum_pool(name="turn_psum", bufs=2))
         mx_psum = ctx.enter_context(tc.psum_pool(name="mx_psum", bufs=2))
@@ -247,35 +247,37 @@ def tile_bloomattention_pa_t_kernel(tc, q, k, hidden_states, w_v, b_v, out):
             live[n] = {"banks": banks}
 
         def row_max(n):
+            b, t, h = units[n]
             banks = live[n]["banks"]
-            tops = small.tile([P, 2], F32)
+            minus_s = score_pool.tile([P, S], F32)
+            lows = small.tile([P, 2], F32)
             for i, (sc, k0, width) in enumerate(banks):
-                nc.vector.tensor_reduce(out=tops[:, i : i + 1], in_=sc[:, :width], axis=AX.X, op=ALU.max)
-            shift = small.tile([P, 1], F32)
-            if len(banks) == 2:
                 nc.vector.tensor_scalar(
-                    out=shift[:], in0=tops[:, 0:1], scalar1=tops[:, 1:2], scalar2=-SCALE, op0=ALU.max, op1=ALU.mult
+                    out=minus_s[:, k0 : k0 + width],
+                    in0=sc[:, :width],
+                    scalar1=-SCALE,
+                    scalar2=(lows[:, i - 1 : i] if i > 0 else None),
+                    op0=ALU.mult,
+                    op1=ALU.min,
+                    accum_out=lows[:, i : i + 1],
                 )
-            else:
-                nc.vector.tensor_scalar(out=shift[:], in0=tops[:, 0:1], scalar1=-SCALE, scalar2=None, op0=ALU.mult)
-            live[n]["shift"] = shift
+            live[n]["minus_s"] = minus_s
+            live[n]["shift"] = lows[:, len(banks) - 1 : len(banks)]
 
         def exponentials(n):
             b, t, h = units[n]
             if h == 0:
-                part_sums = small.tile([P, NH, 2], F32)
-                tile_live[(b, t)] = {"part_sums": part_sums}
-            part_sums = tile_live[(b, t)]["part_sums"]
-            e_tile = e_tiles[(t, h % 2)]
-            for i, (sc, k0, width) in enumerate(live[n]["banks"]):
-                nc.scalar.activation(
-                    out=e_tile[:, k0 : k0 + width],
-                    in_=sc[:, :width],
-                    func=ACT.Exp,
-                    bias=live[n]["shift"][:, 0:1],
-                    scale=SCALE,
-                    accum_out=part_sums[:, h, i : i + 1],
-                )
+                row_sums = small.tile([P, NH], F32)
+                tile_live[(b, t)] = {"row_sums": row_sums}
+            n_keys = (t + 1) * P
+            nc.scalar.activation(
+                out=e_tiles[(t, h % 2)][:, :n_keys],
+                in_=live[n]["minus_s"][:, :n_keys],
+                func=ACT.Exp,
+                bias=live[n]["shift"],
+                scale=-1.0,
+                accum_out=tile_live[(b, t)]["row_sums"][:, h : h + 1],
+            )
 
         def turn(n):
             b, t, h = units[n]
@@ -330,13 +332,8 @@ def tile_bloomattention_pa_t_kernel(tc, q, k, hidden_states, w_v, b_v, out):
             tile_live[(b, t)]["acc"] = acc
 
         def normalise_and_store(b, t):
-            passes = t // 4 + 1
-            row_sum = small.tile([P, NH], F32)
-            nc.vector.tensor_reduce(
-                out=row_sum[:], in_=tile_live[(b, t)]["part_sums"][:, :, :passes], axis=AX.X, op=ALU.add
-            )
             inverse = small.tile([P, NH], F32)
-            nc.vector.reciprocal(inverse[:], row_sum[:])
+            nc.vector.reciprocal(inverse[:], tile_live[(b, t)]["row_sums"][:])
             result = flow.tile([P, NH, D], F32)
             nc.vector.tensor_tensor(
                 out=result[:],

@@ -22,6 +22,11 @@ K_PASS = 512
 SCALE = 1.0 / math.sqrt(D)
 MASKED = -131072.0
 
+HEADS_PER_QUANTISE = 4
+PREP_ON_SCALAR = False
+NORMALISE_ON_SCALAR = False
+TILE_ORDER = (0, 1, 2, 3, 4, 5, 6, 7)
+
 FLOPS = 2 * B * S * H * H + 2 * (2 * B * NH * D * (512 * 512 + 512 * 1024))
 
 
@@ -109,7 +114,7 @@ def tile_bloomattention_pa_t_kernel(tc, q, k, hidden_states, w_v, b_v, out):
                 e_tiles[(t, parity)] = e_tile
 
         def empty_bank(index, dst, src):
-            if index % 2 == 0:
+            if PREP_ON_SCALAR or index % 2 == 0:
                 nc.scalar.copy(out=dst, in_=src)
             else:
                 nc.vector.tensor_copy(out=dst, in_=src)
@@ -293,26 +298,29 @@ def tile_bloomattention_pa_t_kernel(tc, q, k, hidden_states, w_v, b_v, out):
         def regroup(n):
             b, t, h = units[n]
             passes = t // 4 + 1
-            e_grouped = flow.tile([P, 2 * K_PASS], BF16, align_bytes=64)
+            if h == 0:
+                e_grouped = flow.tile([P, NH, passes * K_PASS], BF16, align_bytes=64)
+                tile_live[(b, t)]["e_grouped"] = e_grouped
             nc.scalar.copy(
-                out=e_grouped[:].bitcast(F32)[:, : passes * 2 * P].rearrange("p (g i u) -> p g i u", g=passes, u=2),
+                out=tile_live[(b, t)]["e_grouped"][:, h, :].bitcast(F32).rearrange("p (g i u) -> p g i u", g=passes, u=2),
                 in_=live[n]["turned"][:, :passes, :, :].rearrange("p g u i -> p g i u"),
             )
-            live[n]["e_grouped"] = e_grouped
 
         def quantise(n):
             b, t, h = units[n]
             passes = t // 4 + 1
             if h == 0:
-                e_codes = flow.tile([P, NH, 2 * P], U32, align_bytes=64)
-                e_scales = flow.tile([P, NH, 2 * P], U8, align_bytes=64)
+                e_codes = flow.tile([P, NH, passes * P], U32, align_bytes=64)
+                e_scales = flow.tile([P, NH, passes * P], U8, align_bytes=64)
                 tile_live[(b, t)]["e_codes"] = e_codes
                 tile_live[(b, t)]["e_scales"] = e_scales
-            nc.vector.quantize_mx(
-                out=tile_live[(b, t)]["e_codes"][:, h, : passes * P].bitcast(FP8X4),
-                scales=tile_live[(b, t)]["e_scales"][:, h, : passes * P],
-                in_=live[n]["e_grouped"][:, : passes * K_PASS],
-            )
+            if (h + 1) % HEADS_PER_QUANTISE == 0:
+                heads = slice(h + 1 - HEADS_PER_QUANTISE, h + 1)
+                nc.vector.quantize_mx(
+                    out=tile_live[(b, t)]["e_codes"][:, heads, :].rearrange("p h c -> p (h c)").bitcast(FP8X4),
+                    scales=tile_live[(b, t)]["e_scales"][:, heads, :].rearrange("p h c -> p (h c)"),
+                    in_=tile_live[(b, t)]["e_grouped"][:, heads, :].rearrange("p h c -> p (h c)"),
+                )
 
         def weighted_values(b, t):
             passes = t // 4 + 1

@@ -19,13 +19,10 @@ P = 128
 NT = S // P
 BANK = 512
 K_PASS = 512
+HALF = S // 2
 SCALE = 1.0 / math.sqrt(D)
 MASKED = -131072.0
-
-HEADS_PER_QUANTISE = 4
-PREP_ON_SCALAR = False
-NORMALISE_ON_SCALAR = False
-TILE_ORDER = (0, 1, 2, 3, 4, 5, 6, 7)
+MANUAL = True
 
 FLOPS = 2 * B * S * H * H + 2 * (2 * B * NH * D * (512 * 512 + 512 * 1024))
 
@@ -38,31 +35,38 @@ def tile_bloomattention_pa_t_kernel(tc, q, k, hidden_states, w_v, b_v, out):
         batch = ctx.enter_context(tc.tile_pool(name="batch", bufs=2))
         stage = ctx.enter_context(tc.tile_pool(name="stage", bufs=1))
         flow = ctx.enter_context(tc.tile_pool(name="flow", bufs=2))
-        small = ctx.enter_context(tc.tile_pool(name="small", bufs=4))
+        small = ctx.enter_context(tc.tile_pool(name="small", bufs=6))
         score_pool = ctx.enter_context(tc.tile_pool(name="score_pool", bufs=3))
         wide_psum = ctx.enter_context(tc.psum_pool(name="wide_psum", bufs=4))
         turn_psum = ctx.enter_context(tc.psum_pool(name="turn_psum", bufs=2))
         mx_psum = ctx.enter_context(tc.psum_pool(name="mx_psum", bufs=2))
+        if MANUAL:
+            ctx.enter_context(tc.manual_schedule())
 
         loaded = {}
 
-        def load(b):
+        def load_hidden(b):
             hid_raw = raw.tile([P, 8 * H], BF16)
-            k_raw = raw.tile([P, NT * H], BF16)
-            q_raw = raw.tile([P, NT * H], BF16)
             nc.sync.dma_start(
                 out=hid_raw[:].rearrange("p (a x) -> p a x", a=4),
                 in_=hidden_states[b].rearrange("(a p e) f -> p a (e f)", p=P, e=2),
             )
+            loaded[("hid", b)] = hid_raw
+
+        def load_half(what, src, b, half):
+            piece = raw.tile([P, 4 * H], BF16, tag="%s_raw%d" % (what, half))
             nc.sync.dma_start(
-                out=k_raw[:].rearrange("p (t x) -> p t x", t=NT),
-                in_=k[b].rearrange("(t p) h d -> p t (h d)", p=P),
+                out=piece[:].rearrange("p (t x) -> p t x", t=4),
+                in_=src[b, half * HALF : (half + 1) * HALF].rearrange("(t p) h d -> p t (h d)", p=P),
             )
-            nc.sync.dma_start(
-                out=q_raw[:].rearrange("p (t x) -> p t x", t=NT),
-                in_=q[b].rearrange("(t p) h d -> p t (h d)", p=P),
-            )
-            loaded[b] = {"hid": hid_raw, "k": k_raw, "q": q_raw}
+            loaded[(what, b, half)] = piece
+
+        def load(b):
+            load_hidden(b)
+            load_half("k", k, b, 0)
+            load_half("q", q, b, 0)
+            load_half("k", k, b, 1)
+            load_half("q", q, b, 1)
 
         w_raw = const.tile([P, NH * H], BF16)
         nc.sync.dma_start(
@@ -113,11 +117,11 @@ def tile_bloomattention_pa_t_kernel(tc, q, k, hidden_states, w_v, b_v, out):
                     nc.gpsimd.memset(e_tile[:, (t + 1) * P :], 0.0)
                 e_tiles[(t, parity)] = e_tile
 
-        def empty_bank(index, dst, src):
-            if PREP_ON_SCALAR or index % 2 == 0:
-                nc.scalar.copy(out=dst, in_=src)
-            else:
+        def copy_out(on_vector, dst, src):
+            if on_vector:
                 nc.vector.tensor_copy(out=dst, in_=src)
+            else:
+                nc.scalar.copy(out=dst, in_=src)
 
         def turn_words(raw_words, grouped_words, pair):
             bank = wide_psum.tile([P, 2, 2, P], F32, tag="wide")
@@ -126,54 +130,40 @@ def tile_bloomattention_pa_t_kernel(tc, q, k, hidden_states, w_v, b_v, out):
                     first = ((2 * pair + s) * 2 + u) * P
                     nc.tensor.transpose(bank[:, s, u, :], raw_words[:, first : first + P], ident_f32[:])
             return (
-                pair,
                 grouped_words[:, pair * BANK : (pair + 1) * BANK].rearrange("p (s r u) -> p s r u", s=2, u=2),
                 bank[:].rearrange("p s u r -> p s r u"),
             )
 
-        def turn_head(src, dst, h):
-            bank = wide_psum.tile([P, NT, P], BF16, tag="wide")
-            for t in range(NT):
-                first = t * H + h * D
-                nc.tensor.transpose(bank[:, t, :], src[:, first : first + D], ident_bf[:])
-            return (h, dst[:, h, :], bank[:].rearrange("p t r -> p (t r)"))
-
-        w_grouped = const.tile([P, NH * H], BF16, align_bytes=64)
-        w_codes = const.tile([P, H], U32, align_bytes=64)
-        w_scales = const.tile([P, H], U8, align_bytes=64)
-        for pair in range(NH // 2):
-            empty_bank(*turn_words(w_raw[:].bitcast(F32), w_grouped[:].bitcast(F32), pair))
-        nc.vector.quantize_mx(out=w_codes[:].bitcast(FP8X4), scales=w_scales[:], in_=w_grouped[:])
-
         ready = {}
+
+        def turn_half(what, b, half, head_pair):
+            if half == 0 and head_pair == 0:
+                turned_heads = batch.tile([P, NH, S], BF16, tag=what + "T")
+                ready.setdefault(b, {})[what + "T"] = turned_heads
+            bank = wide_psum.tile([P, 2, 4, P], BF16, tag="wide")
+            src = loaded[(what, b, half)]
+            for hh in range(2):
+                for tt in range(4):
+                    first = tt * H + (2 * head_pair + hh) * D
+                    nc.tensor.transpose(bank[:, hh, tt, :], src[:, first : first + D], ident_bf[:])
+            return (
+                ready[b][what + "T"][:, 2 * head_pair : 2 * head_pair + 2, half * HALF : (half + 1) * HALF],
+                bank[:].rearrange("p hh tt r -> p hh (tt r)"),
+            )
 
         def turn_hidden(b, pair):
             if pair == 0:
                 hid_grouped = stage.tile([P, 8 * H], BF16, align_bytes=64)
-                ready[b] = {"hid_grouped": hid_grouped}
-            return turn_words(loaded[b]["hid"][:].bitcast(F32), ready[b]["hid_grouped"][:].bitcast(F32), pair)
-
-        def turn_keys(b, h):
-            if h == 0:
-                kT = batch.tile([P, NH, S], BF16)
-                ready[b]["kT"] = kT
-            return turn_head(loaded[b]["k"], ready[b]["kT"], h)
-
-        def turn_queries(b, h):
-            if h == 0:
-                qT = batch.tile([P, NH, S], BF16)
-                ready[b]["qT"] = qT
-            return turn_head(loaded[b]["q"], ready[b]["qT"], h)
+                ready.setdefault(b, {})["hid_grouped"] = hid_grouped
+            return turn_words(loaded[("hid", b)][:].bitcast(F32), ready[b]["hid_grouped"][:].bitcast(F32), pair)
 
         def quantise_hidden(b):
-            hid_codes = stage.tile([P, 8 * P], U32, align_bytes=64)
-            hid_scales = stage.tile([P, 8 * P], U8, align_bytes=64)
+            hid_codes = batch.tile([P, 8 * P], U32, align_bytes=64)
+            hid_scales = batch.tile([P, 8 * P], U8, align_bytes=64)
             ready[b]["hid_codes"] = hid_codes
             ready[b]["hid_scales"] = hid_scales
             nc.vector.quantize_mx(
-                out=ready[b]["hid_codes"][:].bitcast(FP8X4),
-                scales=ready[b]["hid_scales"][:],
-                in_=ready[b]["hid_grouped"][:],
+                out=hid_codes[:].bitcast(FP8X4), scales=hid_scales[:], in_=ready[b]["hid_grouped"][:]
             )
 
         def project_values(b, g, h):
@@ -190,7 +180,7 @@ def tile_bloomattention_pa_t_kernel(tc, q, k, hidden_states, w_v, b_v, out):
                     start=True,
                     stop=True,
                 )
-            ready[b]["acc"] = acc
+            ready[b][("acc", h)] = acc
 
         def add_bias(b, g, h):
             if h == 0:
@@ -198,23 +188,25 @@ def tile_bloomattention_pa_t_kernel(tc, q, k, hidden_states, w_v, b_v, out):
                 ready[b]["v_grouped"] = v_grouped
             nc.vector.tensor_tensor(
                 out=ready[b]["v_grouped"][:, h, :, :],
-                in0=ready[b]["acc"][:].rearrange("p j d -> p d j"),
+                in0=ready[b][("acc", h)][:].rearrange("p j d -> p d j"),
                 in1=bias_bc[:, h * D : (h + 1) * D].unsqueeze(2).to_broadcast([P, D, 4]),
                 op=ALU.add,
             )
-            if h == NH - 1:
-                if g == 0:
-                    v_codes = batch.tile([P, 2, H], U32, align_bytes=64)
-                    v_scales = batch.tile([P, 2, H], U8, align_bytes=64)
-                    ready[b]["v_codes"] = v_codes
-                    ready[b]["v_scales"] = v_scales
-                nc.vector.quantize_mx(
-                    out=ready[b]["v_codes"][:, g, :].bitcast(FP8X4),
-                    scales=ready[b]["v_scales"][:, g, :],
-                    in_=ready[b]["v_grouped"][:].rearrange("p h d j -> p (h d j)"),
-                )
+
+        def quantise_values(b, g):
+            if g == 0:
+                v_codes = batch.tile([P, 2, H], U32, align_bytes=64)
+                v_scales = batch.tile([P, 2, H], U8, align_bytes=64)
+                ready[b]["v_codes"] = v_codes
+                ready[b]["v_scales"] = v_scales
+            nc.vector.quantize_mx(
+                out=ready[b]["v_codes"][:, g, :].bitcast(FP8X4),
+                scales=ready[b]["v_scales"][:, g, :],
+                in_=ready[b]["v_grouped"][:].rearrange("p h d j -> p (h d j)"),
+            )
 
         units = [(b, t, h) for b in range(B) for t in range(NT) for h in range(NH)]
+        n_units = len(units)
         live = {}
         tile_live = {}
 
@@ -251,8 +243,7 @@ def tile_bloomattention_pa_t_kernel(tc, q, k, hidden_states, w_v, b_v, out):
                 banks.append((sc, k0, width))
             live[n] = {"banks": banks}
 
-        def row_max(n):
-            b, t, h = units[n]
+        def empty_scores(n):
             banks = live[n]["banks"]
             minus_s = score_pool.tile([P, S], F32)
             lows = small.tile([P, 2], F32)
@@ -261,13 +252,20 @@ def tile_bloomattention_pa_t_kernel(tc, q, k, hidden_states, w_v, b_v, out):
                     out=minus_s[:, k0 : k0 + width],
                     in0=sc[:, :width],
                     scalar1=-SCALE,
-                    scalar2=(lows[:, i - 1 : i] if i > 0 else None),
+                    scalar2=None,
                     op0=ALU.mult,
                     op1=ALU.min,
                     accum_out=lows[:, i : i + 1],
                 )
             live[n]["minus_s"] = minus_s
-            live[n]["shift"] = lows[:, len(banks) - 1 : len(banks)]
+            if len(banks) == 2:
+                shift = small.tile([P, 1], F32)
+                nc.gpsimd.tensor_scalar(
+                    out=shift[:], in0=lows[:, 0:1], scalar1=lows[:, 1:2], scalar2=None, op0=ALU.min
+                )
+                live[n]["shift"] = shift[:]
+            else:
+                live[n]["shift"] = lows[:, 0:1]
 
         def exponentials(n):
             b, t, h = units[n]
@@ -306,21 +304,22 @@ def tile_bloomattention_pa_t_kernel(tc, q, k, hidden_states, w_v, b_v, out):
                 in_=live[n]["turned"][:, :passes, :, :].rearrange("p g u i -> p g i u"),
             )
 
-        def quantise(n):
-            b, t, h = units[n]
+        def quantise(b, t):
             passes = t // 4 + 1
-            if h == 0:
-                e_codes = flow.tile([P, NH, passes * P], U32, align_bytes=64)
-                e_scales = flow.tile([P, NH, passes * P], U8, align_bytes=64)
-                tile_live[(b, t)]["e_codes"] = e_codes
-                tile_live[(b, t)]["e_scales"] = e_scales
-            if (h + 1) % HEADS_PER_QUANTISE == 0:
-                heads = slice(h + 1 - HEADS_PER_QUANTISE, h + 1)
-                nc.vector.quantize_mx(
-                    out=tile_live[(b, t)]["e_codes"][:, heads, :].rearrange("p h c -> p (h c)").bitcast(FP8X4),
-                    scales=tile_live[(b, t)]["e_scales"][:, heads, :].rearrange("p h c -> p (h c)"),
-                    in_=tile_live[(b, t)]["e_grouped"][:, heads, :].rearrange("p h c -> p (h c)"),
-                )
+            e_codes = flow.tile([P, NH, passes * P], U32, align_bytes=64)
+            e_scales = flow.tile([P, NH, passes * P], U8, align_bytes=64)
+            tile_live[(b, t)]["e_codes"] = e_codes
+            tile_live[(b, t)]["e_scales"] = e_scales
+            nc.vector.quantize_mx(
+                out=e_codes[:].rearrange("p h c -> p (h c)").bitcast(FP8X4),
+                scales=e_scales[:].rearrange("p h c -> p (h c)"),
+                in_=tile_live[(b, t)]["e_grouped"][:].rearrange("p h c -> p (h c)"),
+            )
+
+        def invert_sums(b, t):
+            inverse = small.tile([P, NH], F32)
+            nc.vector.reciprocal(inverse[:], tile_live[(b, t)]["row_sums"][:])
+            tile_live[(b, t)]["inverse"] = inverse
 
         def weighted_values(b, t):
             passes = t // 4 + 1
@@ -340,65 +339,99 @@ def tile_bloomattention_pa_t_kernel(tc, q, k, hidden_states, w_v, b_v, out):
             tile_live[(b, t)]["acc"] = acc
 
         def normalise_and_store(b, t):
-            inverse = small.tile([P, NH], F32)
-            nc.vector.reciprocal(inverse[:], tile_live[(b, t)]["row_sums"][:])
             result = flow.tile([P, NH, D], F32)
             nc.vector.tensor_tensor(
                 out=result[:],
                 in0=tile_live[(b, t)]["acc"][:],
-                in1=inverse[:].unsqueeze(2).to_broadcast([P, NH, D]),
+                in1=tile_live[(b, t)]["inverse"][:].unsqueeze(2).to_broadcast([P, NH, D]),
                 op=ALU.mult,
             )
             nc.sync.dma_start(out=out[b, t * P : (t + 1) * P, :], in_=result[:].rearrange("p h d -> p (h d)"))
 
-        for pair in range(4):
-            empty_bank(*turn_hidden(0, pair))
-        quantise_hidden(0)
+        w_grouped = const.tile([P, NH * H], BF16, align_bytes=64)
+        w_codes = const.tile([P, H], U32, align_bytes=64)
+        w_scales = const.tile([P, H], U8, align_bytes=64)
+        head_jobs = [lambda pair=pair: turn_words(w_raw[:].bitcast(F32), w_grouped[:].bitcast(F32), pair) for pair in range(2)]
+        head_jobs.extend([lambda pair=pair: turn_hidden(0, pair) for pair in range(4)])
+        head_jobs.extend([lambda hp=hp: turn_half("k", 0, 0, hp) for hp in range(2)])
+        head_jobs.extend([lambda hp=hp: turn_half("q", 0, 0, hp) for hp in range(2)])
+        waiting = None
+        for index, job in enumerate(head_jobs):
+            made = job()
+            if waiting is not None:
+                copy_out(index % 2 == 0, *waiting)
+            waiting = made
+            if index == 3:
+                nc.vector.quantize_mx(out=w_codes[:].bitcast(FP8X4), scales=w_scales[:], in_=w_grouped[:])
+            if index == 7:
+                quantise_hidden(0)
+        copy_out(True, *waiting)
+        waiting = None
+        project_values(0, 0, 0)
         for h in range(NH):
-            empty_bank(*turn_keys(0, h))
-        for h in range(NH):
-            empty_bank(*turn_queries(0, h))
-        for g in range(2):
-            for h in range(NH):
-                project_values(0, g, h)
-                add_bias(0, g, h)
+            if h + 1 < NH:
+                project_values(0, 0, h + 1)
+            add_bias(0, 0, h)
+        quantise_values(0, 0)
 
-        n_units = len(units)
-        for n in range(n_units + 3):
-            closing = n >= 3 and units[n - 3][2] == NH - 1
-            if n >= 3:
-                quantise(n - 3)
-            if 2 <= n < n_units + 2:
-                turn(n - 2)
-            leaving = None
-            if n < n_units:
-                b, t, h = units[n]
-                if b + 2 < B and t == 0 and h == 0:
-                    load(b + 2)
-                if b + 1 < B:
-                    if t == 0:
-                        leaving = turn_hidden(b + 1, h)
-                    if t == 1 and h == 0:
-                        quantise_hidden(b + 1)
-                    if t == 1:
-                        leaving = turn_keys(b + 1, h)
-                    if t == 2:
-                        leaving = turn_queries(b + 1, h)
-                scores(n)
-            if closing:
-                done_b, done_t = units[n - 3][0], units[n - 3][1]
-                weighted_values(done_b, done_t)
-                if done_b + 1 < B:
-                    project_values(done_b + 1, done_t // 4, done_t % 4)
-            if n < n_units:
-                row_max(n)
-            if 1 <= n < n_units + 1:
-                exponentials(n - 1)
-            if 2 <= n < n_units + 2:
-                regroup(n - 2)
-            if closing:
-                normalise_and_store(done_b, done_t)
-                if done_b + 1 < B:
-                    add_bias(done_b + 1, done_t // 4, done_t % 4)
-            if leaving is not None:
-                empty_bank(*leaving)
+        def completed(n):
+            if 0 <= n < n_units and units[n][2] == NH - 1:
+                return (units[n][0], units[n][1])
+            return None
+
+        def projection_of(s):
+            if s < 0 or s % 4 != 1:
+                return None
+            b, i = (s // 4) // 8, (s // 4) % 8
+            if i < 4:
+                return (b, 1, i) if b < B else None
+            return (b + 1, 0, i - 4) if b + 1 < B else None
+
+        def preparation(b, j):
+            if j < 2:
+                return turn_half("k", b, 1, j)
+            if j < 4:
+                return turn_half("q", b, 1, j - 2)
+            if b + 1 >= B or j >= 12:
+                return None
+            if j < 8:
+                return turn_hidden(b + 1, j - 4)
+            if j < 10:
+                return turn_half("k", b + 1, 0, j - 8)
+            return turn_half("q", b + 1, 0, j - 10)
+
+        steps_of_batch = NT * NH
+        for s in range(n_units + 8):
+            b, j = s // steps_of_batch, s % steps_of_batch
+            if 3 <= s < n_units + 3:
+                turn(s - 3)
+            if s < n_units:
+                scores(s)
+            if completed(s - 6) is not None:
+                weighted_values(*completed(s - 6))
+            if projection_of(s) is not None:
+                project_values(*projection_of(s))
+            made = preparation(b, j) if s < n_units else None
+            if 1 <= s < n_units + 1:
+                empty_scores(s - 1)
+            if completed(s - 7) is not None:
+                normalise_and_store(*completed(s - 7))
+            if projection_of(s - 2) is not None:
+                add_bias(*projection_of(s - 2))
+            if completed(s - 5) is not None:
+                quantise(*completed(s - 5))
+            if completed(s - 4) is not None:
+                invert_sums(*completed(s - 4))
+            if projection_of(s - 4) is not None and projection_of(s - 4)[2] == NH - 1:
+                quantise_values(projection_of(s - 4)[0], projection_of(s - 4)[1])
+            if s < n_units and j == 9 and b + 1 < B:
+                quantise_hidden(b + 1)
+            if 2 <= s < n_units + 2:
+                exponentials(s - 2)
+            if 4 <= s < n_units + 4:
+                regroup(s - 4)
+            if waiting is not None:
+                copy_out(False, *waiting)
+            waiting = made
+            if s < n_units and j == 13 and b + 2 < B:
+                load(b + 2)

@@ -111,7 +111,7 @@ def tile_bloomattention_pa_t_kernel(tc, q, k, hidden_states, w_v, b_v, out):
         e_tiles = {}
         for t in range(NT):
             width = K_PASS * (t // 4 + 1)
-            for parity in range(2):
+            for parity in range(3):
                 e_tile = const.tile([P, width], BF16, name="e_%d_%d" % (t, parity))
                 if (t + 1) * P < width:
                     nc.gpsimd.memset(e_tile[:, (t + 1) * P :], 0.0)
@@ -180,15 +180,15 @@ def tile_bloomattention_pa_t_kernel(tc, q, k, hidden_states, w_v, b_v, out):
                     start=True,
                     stop=True,
                 )
-            ready[b][("acc", h)] = acc
+            ready[b][("acc", g, h)] = acc
 
         def add_bias(b, g, h):
             if h == 0:
                 v_grouped = flow.tile([P, NH, D, 4], BF16, align_bytes=64)
-                ready[b]["v_grouped"] = v_grouped
+                ready[b][("v_grouped", g)] = v_grouped
             nc.vector.tensor_tensor(
-                out=ready[b]["v_grouped"][:, h, :, :],
-                in0=ready[b][("acc", h)][:].rearrange("p j d -> p d j"),
+                out=ready[b][("v_grouped", g)][:, h, :, :],
+                in0=ready[b][("acc", g, h)][:].rearrange("p j d -> p d j"),
                 in1=bias_bc[:, h * D : (h + 1) * D].unsqueeze(2).to_broadcast([P, D, 4]),
                 op=ALU.add,
             )
@@ -202,10 +202,12 @@ def tile_bloomattention_pa_t_kernel(tc, q, k, hidden_states, w_v, b_v, out):
             nc.vector.quantize_mx(
                 out=ready[b]["v_codes"][:, g, :].bitcast(FP8X4),
                 scales=ready[b]["v_scales"][:, g, :],
-                in_=ready[b]["v_grouped"][:].rearrange("p h d j -> p (h d j)"),
+                in_=ready[b][("v_grouped", g)][:].rearrange("p h d j -> p (h d j)"),
             )
 
-        units = [(b, t, h) for b in range(B) for t in range(NT) for h in range(NH)]
+        units = [
+            (b, t if b + 1 < B else NT - 1 - t, h) for b in range(B) for t in range(NT) for h in range(NH)
+        ]
         n_units = len(units)
         live = {}
         tile_live = {}
@@ -274,7 +276,7 @@ def tile_bloomattention_pa_t_kernel(tc, q, k, hidden_states, w_v, b_v, out):
                 tile_live[(b, t)] = {"row_sums": row_sums}
             n_keys = (t + 1) * P
             nc.scalar.activation(
-                out=e_tiles[(t, h % 2)][:, :n_keys],
+                out=e_tiles[(t, n % 3)][:, :n_keys],
                 in_=live[n]["minus_s"][:, :n_keys],
                 func=ACT.Exp,
                 bias=live[n]["shift"],
@@ -285,7 +287,7 @@ def tile_bloomattention_pa_t_kernel(tc, q, k, hidden_states, w_v, b_v, out):
         def turn(n):
             b, t, h = units[n]
             passes = t // 4 + 1
-            e_words = e_tiles[(t, h % 2)][:].bitcast(F32)
+            e_words = e_tiles[(t, n % 3)][:].bitcast(F32)
             turned = turn_psum.tile([P, 2, 2, P], F32, tag="turn")
             for g in range(passes):
                 for u in range(2):
@@ -379,59 +381,62 @@ def tile_bloomattention_pa_t_kernel(tc, q, k, hidden_states, w_v, b_v, out):
                 return (units[n][0], units[n][1])
             return None
 
-        def projection_of(s):
-            if s < 0 or s % 4 != 1:
-                return None
-            b, i = (s // 4) // 8, (s // 4) % 8
-            if i < 4:
-                return (b, 1, i) if b < B else None
-            return (b + 1, 0, i - 4) if b + 1 < B else None
+        steps_of_batch = NT * NH
+        pieces = [(b, g, h) for b in range(B) for g in range(2) for h in range(NH)][NH:]
+        extra = [(B - 2) * steps_of_batch + j for j in (12, 16, 20, 24)]
+        slots = sorted([s for s in range(1, n_units) if s % 4 == 2] + extra)
+        project_at, bias_at, quantise_at = {}, {}, {}
+        for piece, s in zip(pieces, slots):
+            project_at[s] = piece
+            bias_at[s + (1 if s in extra else 2)] = piece
+            if piece[2] == NH - 1:
+                quantise_at[s + 4] = piece
 
         def preparation(b, j):
-            if j < 2:
-                return turn_half("k", b, 1, j)
-            if j < 4:
-                return turn_half("q", b, 1, j - 2)
-            if b + 1 >= B or j >= 12:
+            jobs = []
+            if b + 1 < B:
+                jobs.extend([("k", b, 1, 0), ("k", b, 1, 1), ("q", b, 1, 0), ("q", b, 1, 1)])
+                jobs.extend([("hid", b + 1, pair) for pair in range(4)])
+                jobs.extend([("k", b + 1, 0, 0), ("k", b + 1, 0, 1), ("q", b + 1, 0, 0), ("q", b + 1, 0, 1)])
+            if b + 2 == B:
+                jobs.extend([("k", b + 1, 1, 0), ("k", b + 1, 1, 1), ("q", b + 1, 1, 0), ("q", b + 1, 1, 1)])
+            if j >= len(jobs):
                 return None
-            if j < 8:
-                return turn_hidden(b + 1, j - 4)
-            if j < 10:
-                return turn_half("k", b + 1, 0, j - 8)
-            return turn_half("q", b + 1, 0, j - 10)
+            if jobs[j][0] == "hid":
+                return turn_hidden(jobs[j][1], jobs[j][2])
+            return turn_half(*jobs[j])
 
-        steps_of_batch = NT * NH
-        for s in range(n_units + 8):
+        for s in range(n_units + 9):
             b, j = s // steps_of_batch, s % steps_of_batch
-            if 3 <= s < n_units + 3:
-                turn(s - 3)
+            if 4 <= s < n_units + 4:
+                turn(s - 4)
             if s < n_units:
                 scores(s)
-            if completed(s - 6) is not None:
-                weighted_values(*completed(s - 6))
-            if projection_of(s) is not None:
-                project_values(*projection_of(s))
+            if completed(s - 7) is not None:
+                weighted_values(*completed(s - 7))
+            if s in project_at:
+                project_values(*project_at[s])
             made = preparation(b, j) if s < n_units else None
             if 1 <= s < n_units + 1:
                 empty_scores(s - 1)
-            if completed(s - 7) is not None:
-                normalise_and_store(*completed(s - 7))
-            if projection_of(s - 2) is not None:
-                add_bias(*projection_of(s - 2))
-            if completed(s - 5) is not None:
-                quantise(*completed(s - 5))
+            if completed(s - 8) is not None:
+                normalise_and_store(*completed(s - 8))
+            if s in bias_at:
+                add_bias(*bias_at[s])
+            if completed(s - 6) is not None:
+                quantise(*completed(s - 6))
             if completed(s - 4) is not None:
                 invert_sums(*completed(s - 4))
-            if projection_of(s - 4) is not None and projection_of(s - 4)[2] == NH - 1:
-                quantise_values(projection_of(s - 4)[0], projection_of(s - 4)[1])
+            if s in quantise_at:
+                quantise_values(quantise_at[s][0], quantise_at[s][1])
             if s < n_units and j == 9 and b + 1 < B:
                 quantise_hidden(b + 1)
+            if 5 <= s < n_units + 5:
+                regroup(s - 5)
             if 2 <= s < n_units + 2:
                 exponentials(s - 2)
-            if 4 <= s < n_units + 4:
-                regroup(s - 4)
             if waiting is not None:
-                copy_out(False, *waiting)
+                copy_out(s % 2 == 1, *waiting)
             waiting = made
             if s < n_units and j == 13 and b + 2 < B:
                 load(b + 2)

@@ -36,10 +36,8 @@ def tile_bloomattention_pa_t_kernel(tc, q, k, hidden_states, w_v, b_v, out):
         stage = ctx.enter_context(tc.tile_pool(name="stage", bufs=1))
         flow = ctx.enter_context(tc.tile_pool(name="flow", bufs=2))
         small = ctx.enter_context(tc.tile_pool(name="small", bufs=6))
-        score_pool = ctx.enter_context(tc.tile_pool(name="score_pool", bufs=3))
-        wide_psum = ctx.enter_context(tc.psum_pool(name="wide_psum", bufs=4))
-        turn_psum = ctx.enter_context(tc.psum_pool(name="turn_psum", bufs=2))
-        mx_psum = ctx.enter_context(tc.psum_pool(name="mx_psum", bufs=2))
+        score_pool = ctx.enter_context(tc.tile_pool(name="score_pool", bufs=4))
+        psum = ctx.enter_context(tc.psum_pool(name="psum", bufs=8))
         if MANUAL:
             ctx.enter_context(tc.manual_schedule())
 
@@ -68,14 +66,17 @@ def tile_bloomattention_pa_t_kernel(tc, q, k, hidden_states, w_v, b_v, out):
             load_half("k", k, b, 1)
             load_half("q", q, b, 1)
 
+        bias_bc = const.tile([P, H], BF16)
+        nc.scalar.dma_start(out=bias_bc[:], in_=b_v.partition_broadcast(P))
+        warm = const.tile([P, 2], F32)
+        nc.vector.memset(warm[:, 0:1], 0.0)
+        nc.scalar.activation(out=warm[:, 1:2], in_=warm[:, 0:1], func=ACT.Exp)
         w_raw = const.tile([P, NH * H], BF16)
         nc.sync.dma_start(
             out=w_raw[:].rearrange("p (r f) -> p r f", r=NH),
             in_=w_v.rearrange("(r p) f -> p r f", p=P),
         )
         load(0)
-        bias_bc = const.tile([P, H], BF16)
-        nc.sync.dma_start(out=bias_bc[:], in_=b_v.partition_broadcast(P))
         load(1)
 
         ident_f32 = const.tile([P, P], F32)
@@ -124,7 +125,7 @@ def tile_bloomattention_pa_t_kernel(tc, q, k, hidden_states, w_v, b_v, out):
                 nc.scalar.copy(out=dst, in_=src)
 
         def turn_words(raw_words, grouped_words, pair):
-            bank = wide_psum.tile([P, 2, 2, P], F32, tag="wide")
+            bank = psum.tile([P, 2, 2, P], F32, tag="bank")
             for s in range(2):
                 for u in range(2):
                     first = ((2 * pair + s) * 2 + u) * P
@@ -140,7 +141,7 @@ def tile_bloomattention_pa_t_kernel(tc, q, k, hidden_states, w_v, b_v, out):
             if half == 0 and head_pair == 0:
                 turned_heads = batch.tile([P, NH, S], BF16, tag=what + "T")
                 ready.setdefault(b, {})[what + "T"] = turned_heads
-            bank = wide_psum.tile([P, 2, 4, P], BF16, tag="wide")
+            bank = psum.tile([P, 2, 4, P], BF16, tag="bank")
             src = loaded[(what, b, half)]
             for hh in range(2):
                 for tt in range(4):
@@ -167,7 +168,7 @@ def tile_bloomattention_pa_t_kernel(tc, q, k, hidden_states, w_v, b_v, out):
             )
 
         def project_values(b, g, h):
-            acc = mx_psum.tile([P, 4, D], F32, tag="mx")
+            acc = psum.tile([P, 4, D], F32, tag="bank")
             cols = slice(h * D, (h + 1) * D)
             for j in range(4):
                 rows = slice((4 * g + j) * P, (4 * g + j + 1) * P)
@@ -220,7 +221,7 @@ def tile_bloomattention_pa_t_kernel(tc, q, k, hidden_states, w_v, b_v, out):
             b, t, h = units[n]
             banks = []
             for k0, width in key_banks(t):
-                sc = wide_psum.tile([P, BANK], F32, tag="wide")
+                sc = psum.tile([P, BANK], F32, tag="bank")
                 for c0 in range(0, width, P):
                     dist = t - (k0 + c0) // P
                     if dist == 0:
@@ -288,7 +289,7 @@ def tile_bloomattention_pa_t_kernel(tc, q, k, hidden_states, w_v, b_v, out):
             b, t, h = units[n]
             passes = t // 4 + 1
             e_words = e_tiles[(t, n % 3)][:].bitcast(F32)
-            turned = turn_psum.tile([P, 2, 2, P], F32, tag="turn")
+            turned = psum.tile([P, 2, 2, P], F32, tag="bank")
             for g in range(passes):
                 for u in range(2):
                     first = (2 * g + u) * P
@@ -326,7 +327,7 @@ def tile_bloomattention_pa_t_kernel(tc, q, k, hidden_states, w_v, b_v, out):
         def weighted_values(b, t):
             passes = t // 4 + 1
             e_codes, e_scales = tile_live[(b, t)]["e_codes"], tile_live[(b, t)]["e_scales"]
-            acc = mx_psum.tile([P, NH, D], F32, tag="mx")
+            acc = psum.tile([P, NH, D], F32, tag="bank")
             for h in range(NH):
                 for g in range(passes):
                     nc.tensor.matmul_mx(
@@ -369,12 +370,8 @@ def tile_bloomattention_pa_t_kernel(tc, q, k, hidden_states, w_v, b_v, out):
                 quantise_hidden(0)
         copy_out(True, *waiting)
         waiting = None
-        project_values(0, 0, 0)
         for h in range(NH):
-            if h + 1 < NH:
-                project_values(0, 0, h + 1)
-            add_bias(0, 0, h)
-        quantise_values(0, 0)
+            project_values(0, 0, h)
 
         def completed(n):
             if 0 <= n < n_units and units[n][2] == NH - 1:
@@ -385,10 +382,11 @@ def tile_bloomattention_pa_t_kernel(tc, q, k, hidden_states, w_v, b_v, out):
         pieces = [(b, g, h) for b in range(B) for g in range(2) for h in range(NH)][NH:]
         extra = [(B - 2) * steps_of_batch + j for j in (12, 16, 20, 24)]
         slots = sorted([s for s in range(1, n_units) if s % 4 == 2] + extra)
-        project_at, bias_at, quantise_at = {}, {}, {}
+        project_at, quantise_at = {}, {6: (0, 0, NH - 1)}
+        bias_at = {h + 1: [(0, 0, h)] for h in range(NH)}
         for piece, s in zip(pieces, slots):
             project_at[s] = piece
-            bias_at[s + (1 if s in extra else 2)] = piece
+            bias_at.setdefault(s + (1 if s in extra else 2), []).append(piece)
             if piece[2] == NH - 1:
                 quantise_at[s + 4] = piece
 
@@ -421,8 +419,8 @@ def tile_bloomattention_pa_t_kernel(tc, q, k, hidden_states, w_v, b_v, out):
                 empty_scores(s - 1)
             if completed(s - 8) is not None:
                 normalise_and_store(*completed(s - 8))
-            if s in bias_at:
-                add_bias(*bias_at[s])
+            for piece in bias_at.get(s, []):
+                add_bias(*piece)
             if completed(s - 6) is not None:
                 quantise(*completed(s - 6))
             if completed(s - 4) is not None:
@@ -436,7 +434,7 @@ def tile_bloomattention_pa_t_kernel(tc, q, k, hidden_states, w_v, b_v, out):
             if 2 <= s < n_units + 2:
                 exponentials(s - 2)
             if waiting is not None:
-                copy_out(s % 2 == 1, *waiting)
+                copy_out(False, *waiting)
             waiting = made
             if s < n_units and j == 13 and b + 2 < B:
                 load(b + 2)

@@ -71,12 +71,16 @@ def tile_bloomattention_pa_t_kernel(tc, q, k, hidden_states, w_v, b_v, out):
         warm = const.tile([P, 2], F32)
         nc.vector.memset(warm[:, 0:1], 0.0)
         nc.scalar.activation(out=warm[:, 1:2], in_=warm[:, 0:1], func=ACT.Exp)
+        load_half("k", k, 0, 0)
+        load_half("q", q, 0, 0)
         w_raw = const.tile([P, NH * H], BF16)
         nc.sync.dma_start(
             out=w_raw[:].rearrange("p (r f) -> p r f", r=NH),
             in_=w_v.rearrange("(r p) f -> p r f", p=P),
         )
-        load(0)
+        load_hidden(0)
+        load_half("k", k, 0, 1)
+        load_half("q", q, 0, 1)
         load(1)
 
         ident_f32 = const.tile([P, P], F32)
@@ -287,14 +291,18 @@ def tile_bloomattention_pa_t_kernel(tc, q, k, hidden_states, w_v, b_v, out):
 
         def turn(n):
             b, t, h = units[n]
-            passes = t // 4 + 1
             e_words = e_tiles[(t, n % 3)][:].bitcast(F32)
-            turned = psum.tile([P, 2, 2, P], F32, tag="bank")
-            for g in range(passes):
+            if t >= 4 or h % 2 == 0:
+                turned = psum.tile([P, 2, 2, P], F32, tag="bank")
+                live[n]["turned"] = turned
+            else:
+                live[n]["turned"] = live[n - 1]["turned"]
+            for g in range(t // 4 + 1):
                 for u in range(2):
                     first = (2 * g + u) * P
-                    nc.tensor.transpose(turned[:, g, u, :], e_words[:, first : first + P], ident_f32[:])
-            live[n]["turned"] = turned
+                    nc.tensor.transpose(
+                        live[n]["turned"][:, g if t >= 4 else h % 2, u, :], e_words[:, first : first + P], ident_f32[:]
+                    )
 
         def regroup(n):
             b, t, h = units[n]
@@ -302,9 +310,15 @@ def tile_bloomattention_pa_t_kernel(tc, q, k, hidden_states, w_v, b_v, out):
             if h == 0:
                 e_grouped = flow.tile([P, NH, passes * K_PASS], BF16, align_bytes=64)
                 tile_live[(b, t)]["e_grouped"] = e_grouped
+            if t < 4 and h % 2 == 0:
+                return
+            heads = slice(h, h + 1) if t >= 4 else slice(h - 1, h + 1)
             nc.scalar.copy(
-                out=tile_live[(b, t)]["e_grouped"][:, h, :].bitcast(F32).rearrange("p (g i u) -> p g i u", g=passes, u=2),
-                in_=live[n]["turned"][:, :passes, :, :].rearrange("p g u i -> p g i u"),
+                out=tile_live[(b, t)]["e_grouped"][:, heads, :]
+                .rearrange("p h c -> p (h c)")
+                .bitcast(F32)
+                .rearrange("p (g i u) -> p g i u", g=2, u=2),
+                in_=live[n]["turned"][:].rearrange("p g u i -> p g i u"),
             )
 
         def quantise(b, t):
@@ -354,55 +368,61 @@ def tile_bloomattention_pa_t_kernel(tc, q, k, hidden_states, w_v, b_v, out):
         w_grouped = const.tile([P, NH * H], BF16, align_bytes=64)
         w_codes = const.tile([P, H], U32, align_bytes=64)
         w_scales = const.tile([P, H], U8, align_bytes=64)
-        head_jobs = [lambda pair=pair: turn_words(w_raw[:].bitcast(F32), w_grouped[:].bitcast(F32), pair) for pair in range(2)]
-        head_jobs.extend([lambda pair=pair: turn_hidden(0, pair) for pair in range(4)])
-        head_jobs.extend([lambda hp=hp: turn_half("k", 0, 0, hp) for hp in range(2)])
-        head_jobs.extend([lambda hp=hp: turn_half("q", 0, 0, hp) for hp in range(2)])
-        waiting = None
-        for index, job in enumerate(head_jobs):
-            made = job()
-            if waiting is not None:
-                copy_out(index % 2 == 0, *waiting)
-            waiting = made
-            if index == 3:
-                nc.vector.quantize_mx(out=w_codes[:].bitcast(FP8X4), scales=w_scales[:], in_=w_grouped[:])
-            if index == 7:
-                quantise_hidden(0)
-        copy_out(True, *waiting)
-        waiting = None
-        for h in range(NH):
-            project_values(0, 0, h)
+
+        def turn_job(job):
+            if job[0] == "w":
+                return turn_words(w_raw[:].bitcast(F32), w_grouped[:].bitcast(F32), job[1])
+            if job[0] == "hid":
+                return turn_hidden(job[1], job[2])
+            return turn_half(*job)
+
+        waiting = []
+        for index, job in enumerate([("k", 0, 0, 0), ("q", 0, 0, 0), ("k", 0, 0, 1), ("q", 0, 0, 1)]):
+            made = turn_job(job)
+            for dst, src in waiting:
+                copy_out(index % 2 == 0, dst, src)
+            waiting = [made]
+
+        steps_of_batch = NT * NH
+        turn_at, hidden_at, project_at, bias_at, quantise_at, mx_at = {}, {}, {}, {}, {}, {}
+
+        def plan(table, s, what):
+            table.setdefault(s, []).append(what)
+
+        for s, job in ((0, ("w", 0)), (0, ("w", 1)), (3, ("hid", 0, 0)), (3, ("hid", 0, 1)), (4, ("hid", 0, 2)), (4, ("hid", 0, 3))):
+            plan(turn_at, s, job)
+        plan(hidden_at, 6, 0)
+        for b in range(B - 1):
+            first = b * steps_of_batch + (5 if b == 0 else 0)
+            jobs = [("k", b, 1, 0), ("k", b, 1, 1), ("q", b, 1, 0), ("q", b, 1, 1)]
+            jobs.extend([("hid", b + 1, pair) for pair in range(4)])
+            jobs.extend([("k", b + 1, 0, 0), ("k", b + 1, 0, 1), ("q", b + 1, 0, 0), ("q", b + 1, 0, 1)])
+            if b + 2 == B:
+                jobs.extend([("k", b + 1, 1, 0), ("k", b + 1, 1, 1), ("q", b + 1, 1, 0), ("q", b + 1, 1, 1)])
+            for i, job in enumerate(jobs):
+                plan(turn_at, first + i, job)
+            plan(hidden_at, first + 9, b + 1)
+
+        pieces = [(b, g, h) for b in range(B) for g in range(2) for h in range(NH)]
+        for i, piece in enumerate(pieces[:NH]):
+            plan(project_at, 7, piece)
+            plan(bias_at, 8 + i // 2, piece)
+        plan(quantise_at, 11, (0, 0))
+        extra = [12] + [(B - 2) * steps_of_batch + j for j in (12, 16, 20, 24)]
+        slots = sorted([s for s in range(10, n_units) if s % 4 == 2] + extra)
+        for piece, s in zip(pieces[NH:], slots):
+            plan(project_at, s, piece)
+            plan(bias_at, s + (1 if s in extra else 2), piece)
+            if piece[2] == NH - 1:
+                plan(quantise_at, s + 4, (piece[0], piece[1]))
+
+        for n in range(NH - 1, n_units, NH):
+            plan(mx_at, max(n + 7, 2 * NH - 1 + 7), (units[n][0], units[n][1]))
 
         def completed(n):
             if 0 <= n < n_units and units[n][2] == NH - 1:
                 return (units[n][0], units[n][1])
             return None
-
-        steps_of_batch = NT * NH
-        pieces = [(b, g, h) for b in range(B) for g in range(2) for h in range(NH)][NH:]
-        extra = [(B - 2) * steps_of_batch + j for j in (12, 16, 20, 24)]
-        slots = sorted([s for s in range(1, n_units) if s % 4 == 2] + extra)
-        project_at, quantise_at = {}, {6: (0, 0, NH - 1)}
-        bias_at = {h + 1: [(0, 0, h)] for h in range(NH)}
-        for piece, s in zip(pieces, slots):
-            project_at[s] = piece
-            bias_at.setdefault(s + (1 if s in extra else 2), []).append(piece)
-            if piece[2] == NH - 1:
-                quantise_at[s + 4] = piece
-
-        def preparation(b, j):
-            jobs = []
-            if b + 1 < B:
-                jobs.extend([("k", b, 1, 0), ("k", b, 1, 1), ("q", b, 1, 0), ("q", b, 1, 1)])
-                jobs.extend([("hid", b + 1, pair) for pair in range(4)])
-                jobs.extend([("k", b + 1, 0, 0), ("k", b + 1, 0, 1), ("q", b + 1, 0, 0), ("q", b + 1, 0, 1)])
-            if b + 2 == B:
-                jobs.extend([("k", b + 1, 1, 0), ("k", b + 1, 1, 1), ("q", b + 1, 1, 0), ("q", b + 1, 1, 1)])
-            if j >= len(jobs):
-                return None
-            if jobs[j][0] == "hid":
-                return turn_hidden(jobs[j][1], jobs[j][2])
-            return turn_half(*jobs[j])
 
         for s in range(n_units + 9):
             b, j = s // steps_of_batch, s % steps_of_batch
@@ -410,31 +430,33 @@ def tile_bloomattention_pa_t_kernel(tc, q, k, hidden_states, w_v, b_v, out):
                 turn(s - 4)
             if s < n_units:
                 scores(s)
-            if completed(s - 7) is not None:
-                weighted_values(*completed(s - 7))
-            if s in project_at:
-                project_values(*project_at[s])
-            made = preparation(b, j) if s < n_units else None
+            for tile_done in mx_at.get(s, []):
+                weighted_values(*tile_done)
+            for piece in project_at.get(s, []):
+                project_values(*piece)
+            made = [turn_job(job) for job in turn_at.get(s, [])]
             if 1 <= s < n_units + 1:
                 empty_scores(s - 1)
-            if completed(s - 8) is not None:
-                normalise_and_store(*completed(s - 8))
+            for tile_done in mx_at.get(s - 1, []):
+                normalise_and_store(*tile_done)
             for piece in bias_at.get(s, []):
                 add_bias(*piece)
             if completed(s - 6) is not None:
                 quantise(*completed(s - 6))
             if completed(s - 4) is not None:
                 invert_sums(*completed(s - 4))
-            if s in quantise_at:
-                quantise_values(quantise_at[s][0], quantise_at[s][1])
-            if s < n_units and j == 9 and b + 1 < B:
-                quantise_hidden(b + 1)
+            for b_g in quantise_at.get(s, []):
+                quantise_values(*b_g)
+            if s == 2:
+                nc.vector.quantize_mx(out=w_codes[:].bitcast(FP8X4), scales=w_scales[:], in_=w_grouped[:])
+            for next_b in hidden_at.get(s, []):
+                quantise_hidden(next_b)
             if 5 <= s < n_units + 5:
                 regroup(s - 5)
             if 2 <= s < n_units + 2:
                 exponentials(s - 2)
-            if waiting is not None:
-                copy_out(False, *waiting)
+            for index, (dst, src) in enumerate(waiting):
+                copy_out(index == 1, dst, src)
             waiting = made
             if s < n_units and j == 13 and b + 2 < B:
                 load(b + 2)

@@ -36,6 +36,7 @@ def tile_bloomattention_pa_t_kernel(tc, q, k, hidden_states, w_v, b_v, out):
         stage = ctx.enter_context(tc.tile_pool(name="stage", bufs=1))
         flow = ctx.enter_context(tc.tile_pool(name="flow", bufs=2))
         small = ctx.enter_context(tc.tile_pool(name="small", bufs=6))
+        results = ctx.enter_context(tc.tile_pool(name="results", bufs=4))
         score_pool = ctx.enter_context(tc.tile_pool(name="score_pool", bufs=4))
         psum = ctx.enter_context(tc.psum_pool(name="psum", bufs=8))
         if MANUAL:
@@ -356,7 +357,7 @@ def tile_bloomattention_pa_t_kernel(tc, q, k, hidden_states, w_v, b_v, out):
             tile_live[(b, t)]["acc"] = acc
 
         def normalise_and_store(b, t):
-            result = flow.tile([P, NH, D], F32)
+            result = results.tile([P, NH, D], F32)
             nc.vector.tensor_tensor(
                 out=result[:],
                 in0=tile_live[(b, t)]["acc"][:],
@@ -458,5 +459,8 @@ def tile_bloomattention_pa_t_kernel(tc, q, k, hidden_states, w_v, b_v, out):
             for index, (dst, src) in enumerate(waiting):
                 copy_out(index == 1, dst, src)
             waiting = made
-            if s < n_units and j == 13 and b + 2 < B:
-                load(b + 2)
+            if s < n_units and b + 2 < B:
+                if j == 13:
+                    load_hidden(b + 2)
+                if j in (15, 17, 19, 21):
+                    load_half("kq"[(j - 15) // 2 % 2], (k, q)[(j - 15) // 2 % 2], b + 2, (j - 15) // 4)

import math
from contextlib import ExitStack

import concourse.mybir as mybir
from concourse.masks import make_identity

BF16 = mybir.dt.bfloat16
F32 = mybir.dt.float32
I32 = mybir.dt.int32
U32 = mybir.dt.uint32
U8 = mybir.dt.uint8
FP8X4 = mybir.dt.float8_e4m3fn_x4
ALU = mybir.AluOpType
ACT = mybir.ActivationFunctionType

B, S, H, NH = 4, 1024, 512, 4
D = H // NH
P = 128
NT = S // P
BANK = 512
K_PASS = 512
HALF = S // 2
SCALE = 1.0 / math.sqrt(D)
MASKED = -131072.0
MANUAL = True

FLOPS = 2 * B * S * H * H + 2 * (2 * B * NH * D * (512 * 512 + 512 * 1024))


def tile_bloomattention_pa_t_kernel(tc, q, k, hidden_states, w_v, b_v, out):
    nc = tc.nc
    with ExitStack() as ctx:
        const = ctx.enter_context(tc.tile_pool(name="const", bufs=1))
        raw = ctx.enter_context(tc.tile_pool(name="raw", bufs=2))
        batch = ctx.enter_context(tc.tile_pool(name="batch", bufs=2))
        stage = ctx.enter_context(tc.tile_pool(name="stage", bufs=1))
        flow = ctx.enter_context(tc.tile_pool(name="flow", bufs=2))
        small = ctx.enter_context(tc.tile_pool(name="small", bufs=6))
        results = ctx.enter_context(tc.tile_pool(name="results", bufs=4))
        score_pool = ctx.enter_context(tc.tile_pool(name="score_pool", bufs=4))
        psum = ctx.enter_context(tc.psum_pool(name="psum", bufs=8))
        if MANUAL:
            ctx.enter_context(tc.manual_schedule())

        loaded = {}

        def load_hidden(b):
            hid_raw = raw.tile([P, 8 * H], BF16)
            nc.sync.dma_start(
                out=hid_raw[:].rearrange("p (a x) -> p a x", a=4),
                in_=hidden_states[b].rearrange("(a p e) f -> p a (e f)", p=P, e=2),
            )
            loaded[("hid", b)] = hid_raw

        def load_half(what, src, b, half):
            piece = raw.tile([P, 4 * H], BF16, tag="%s_raw%d" % (what, half))
            nc.sync.dma_start(
                out=piece[:].rearrange("p (t x) -> p t x", t=4),
                in_=src[b, half * HALF : (half + 1) * HALF].rearrange("(t p) h d -> p t (h d)", p=P),
            )
            loaded[(what, b, half)] = piece

        def load(b):
            load_hidden(b)
            load_half("k", k, b, 0)
            load_half("q", q, b, 0)
            load_half("k", k, b, 1)
            load_half("q", q, b, 1)

        bias_bc = const.tile([P, H], BF16)
        nc.scalar.dma_start(out=bias_bc[:], in_=b_v.partition_broadcast(P))
        warm = const.tile([P, 2], F32)
        nc.vector.memset(warm[:, 0:1], 0.0)
        nc.scalar.activation(out=warm[:, 1:2], in_=warm[:, 0:1], func=ACT.Exp)
        load_half("k", k, 0, 0)
        load_half("q", q, 0, 0)
        w_raw = const.tile([P, NH * H], BF16)
        nc.sync.dma_start(
            out=w_raw[:].rearrange("p (r f) -> p r f", r=NH),
            in_=w_v.rearrange("(r p) f -> p r f", p=P),
        )
        load_hidden(0)
        load_half("k", k, 0, 1)
        load_half("q", q, 0, 1)
        load(1)

        ident_f32 = const.tile([P, P], F32)
        make_identity(nc, ident_f32[:])
        ident_bf = const.tile([P, P], BF16)
        make_identity(nc, ident_bf[:])

        steps = const.tile([P, NT], I32)
        nc.gpsimd.iota(steps[:], pattern=[[-P, NT]], base=1 - P, channel_multiplier=1)
        after = const.tile([P, P], F32)
        nc.gpsimd.memset(after[:], 0.0)
        nc.gpsimd.affine_select(
            out=after[:],
            in_=after[:],
            compare_op=ALU.is_ge,
            fill=MASKED,
            base=0,
            pattern=[[1, P]],
            channel_multiplier=-1,
        )
        slope_col = const.tile([P, NH, NT], F32)
        diag_bias = {}
        for h in range(NH):
            slope = 0.25 ** (h + 1)
            nc.vector.tensor_scalar(
                out=slope_col[:, h, :], in0=steps[:], scalar1=slope / SCALE, scalar2=None, op0=ALU.mult
            )
            diag_bias[h] = const.tile([P, P], F32, name="diag_bias%d" % h)
            nc.vector.tensor_scalar(
                out=diag_bias[h][:], in0=after[:], scalar1=slope_col[:, h, 0:1], scalar2=None, op0=ALU.add
            )

        e_tiles = {}
        for t in range(NT):
            width = K_PASS * (t // 4 + 1)
            for parity in range(3):
                e_tile = const.tile([P, width], BF16, name="e_%d_%d" % (t, parity))
                if (t + 1) * P < width:
                    nc.gpsimd.memset(e_tile[:, (t + 1) * P :], 0.0)
                e_tiles[(t, parity)] = e_tile

        def copy_out(on_vector, dst, src):
            if on_vector:
                nc.vector.tensor_copy(out=dst, in_=src)
            else:
                nc.scalar.copy(out=dst, in_=src)

        def turn_words(raw_words, grouped_words, pair):
            bank = psum.tile([P, 2, 2, P], F32, tag="bank")
            for s in range(2):
                for u in range(2):
                    first = ((2 * pair + s) * 2 + u) * P
                    nc.tensor.transpose(bank[:, s, u, :], raw_words[:, first : first + P], ident_f32[:])
            return (
                grouped_words[:, pair * BANK : (pair + 1) * BANK].rearrange("p (s r u) -> p s r u", s=2, u=2),
                bank[:].rearrange("p s u r -> p s r u"),
            )

        ready = {}

        def turn_half(what, b, half, head_pair):
            if half == 0 and head_pair == 0:
                turned_heads = batch.tile([P, NH, S], BF16, tag=what + "T")
                ready.setdefault(b, {})[what + "T"] = turned_heads
            bank = psum.tile([P, 2, 4, P], BF16, tag="bank")
            src = loaded[(what, b, half)]
            for hh in range(2):
                for tt in range(4):
                    first = tt * H + (2 * head_pair + hh) * D
                    nc.tensor.transpose(bank[:, hh, tt, :], src[:, first : first + D], ident_bf[:])
            return (
                ready[b][what + "T"][:, 2 * head_pair : 2 * head_pair + 2, half * HALF : (half + 1) * HALF],
                bank[:].rearrange("p hh tt r -> p hh (tt r)"),
            )

        def turn_hidden(b, pair):
            if pair == 0:
                hid_grouped = stage.tile([P, 8 * H], BF16, align_bytes=64)
                ready.setdefault(b, {})["hid_grouped"] = hid_grouped
            return turn_words(loaded[("hid", b)][:].bitcast(F32), ready[b]["hid_grouped"][:].bitcast(F32), pair)

        def quantise_hidden(b):
            hid_codes = batch.tile([P, 8 * P], U32, align_bytes=64)
            hid_scales = batch.tile([P, 8 * P], U8, align_bytes=64)
            ready[b]["hid_codes"] = hid_codes
            ready[b]["hid_scales"] = hid_scales
            nc.vector.quantize_mx(
                out=hid_codes[:].bitcast(FP8X4), scales=hid_scales[:], in_=ready[b]["hid_grouped"][:]
            )

        def project_values(b, g, h):
            acc = psum.tile([P, 4, D], F32, tag="bank")
            cols = slice(h * D, (h + 1) * D)
            for j in range(4):
                rows = slice((4 * g + j) * P, (4 * g + j + 1) * P)
                nc.tensor.matmul_mx(
                    out=acc[:, j, :],
                    lhsT=ready[b]["hid_codes"][:, rows].bitcast(FP8X4),
                    lhsT_scale=ready[b]["hid_scales"][:, rows],
                    rhs=w_codes[:, cols].bitcast(FP8X4),
                    rhs_scale=w_scales[:, cols],
                    start=True,
                    stop=True,
                )
            ready[b][("acc", g, h)] = acc

        def add_bias(b, g, h):
            if h == 0:
                v_grouped = flow.tile([P, NH, D, 4], BF16, align_bytes=64)
                ready[b][("v_grouped", g)] = v_grouped
            nc.vector.tensor_tensor(
                out=ready[b][("v_grouped", g)][:, h, :, :],
                in0=ready[b][("acc", g, h)][:].rearrange("p j d -> p d j"),
                in1=bias_bc[:, h * D : (h + 1) * D].unsqueeze(2).to_broadcast([P, D, 4]),
                op=ALU.add,
            )

        def quantise_values(b, g):
            if g == 0:
                v_codes = batch.tile([P, 2, H], U32, align_bytes=64)
                v_scales = batch.tile([P, 2, H], U8, align_bytes=64)
                ready[b]["v_codes"] = v_codes
                ready[b]["v_scales"] = v_scales
            nc.vector.quantize_mx(
                out=ready[b]["v_codes"][:, g, :].bitcast(FP8X4),
                scales=ready[b]["v_scales"][:, g, :],
                in_=ready[b][("v_grouped", g)][:].rearrange("p h d j -> p (h d j)"),
            )

        units = [
            (b, t if b + 1 < B else NT - 1 - t, h) for b in range(B) for t in range(NT) for h in range(NH)
        ]
        n_units = len(units)
        live = {}
        tile_live = {}

        def key_banks(t):
            n_keys = (t + 1) * P
            return [(k0, min(BANK, n_keys - k0)) for k0 in range(0, n_keys, BANK)]

        def scores(n):
            b, t, h = units[n]
            banks = []
            for k0, width in key_banks(t):
                sc = psum.tile([P, BANK], F32, tag="bank")
                for c0 in range(0, width, P):
                    dist = t - (k0 + c0) // P
                    if dist == 0:
                        added = diag_bias[h][:]
                    else:
                        added = slope_col[:, h, dist : dist + 1].to_broadcast([P, P])
                    nc.tensor.matmul(
                        out=sc[:, c0 : c0 + P],
                        lhsT=added,
                        rhs=ident_f32[:],
                        is_transpose=True,
                        start=(c0 == 0),
                        stop=False,
                    )
                nc.tensor.matmul(
                    out=sc[:, :width],
                    lhsT=ready[b]["qT"][:, h, t * P : (t + 1) * P],
                    rhs=ready[b]["kT"][:, h, k0 : k0 + width],
                    start=False,
                    stop=True,
                )
                banks.append((sc, k0, width))
            live[n] = {"banks": banks}

        def empty_scores(n):
            banks = live[n]["banks"]
            minus_s = score_pool.tile([P, S], F32)
            lows = small.tile([P, 2], F32)
            for i, (sc, k0, width) in enumerate(banks):
                nc.vector.tensor_scalar(
                    out=minus_s[:, k0 : k0 + width],
                    in0=sc[:, :width],
                    scalar1=-SCALE,
                    scalar2=None,
                    op0=ALU.mult,
                    op1=ALU.min,
                    accum_out=lows[:, i : i + 1],
                )
            live[n]["minus_s"] = minus_s
            if len(banks) == 2:
                shift = small.tile([P, 1], F32)
                nc.gpsimd.tensor_scalar(
                    out=shift[:], in0=lows[:, 0:1], scalar1=lows[:, 1:2], scalar2=None, op0=ALU.min
                )
                live[n]["shift"] = shift[:]
            else:
                live[n]["shift"] = lows[:, 0:1]

        def exponentials(n):
            b, t, h = units[n]
            if h == 0:
                row_sums = small.tile([P, NH], F32)
                tile_live[(b, t)] = {"row_sums": row_sums}
            n_keys = (t + 1) * P
            nc.scalar.activation(
                out=e_tiles[(t, n % 3)][:, :n_keys],
                in_=live[n]["minus_s"][:, :n_keys],
                func=ACT.Exp,
                bias=live[n]["shift"],
                scale=-1.0,
                accum_out=tile_live[(b, t)]["row_sums"][:, h : h + 1],
            )

        def turn(n):
            b, t, h = units[n]
            e_words = e_tiles[(t, n % 3)][:].bitcast(F32)
            if t >= 4 or h % 2 == 0:
                turned = psum.tile([P, 2, 2, P], F32, tag="bank")
                live[n]["turned"] = turned
            else:
                live[n]["turned"] = live[n - 1]["turned"]
            for g in range(t // 4 + 1):
                for u in range(2):
                    first = (2 * g + u) * P
                    nc.tensor.transpose(
                        live[n]["turned"][:, g if t >= 4 else h % 2, u, :], e_words[:, first : first + P], ident_f32[:]
                    )

        def regroup(n):
            b, t, h = units[n]
            passes = t // 4 + 1
            if h == 0:
                e_grouped = flow.tile([P, NH, passes * K_PASS], BF16, align_bytes=64)
                tile_live[(b, t)]["e_grouped"] = e_grouped
            if t < 4 and h % 2 == 0:
                return
            heads = slice(h, h + 1) if t >= 4 else slice(h - 1, h + 1)
            nc.scalar.copy(
                out=tile_live[(b, t)]["e_grouped"][:, heads, :]
                .rearrange("p h c -> p (h c)")
                .bitcast(F32)
                .rearrange("p (g i u) -> p g i u", g=2, u=2),
                in_=live[n]["turned"][:].rearrange("p g u i -> p g i u"),
            )

        def quantise(b, t):
            passes = t // 4 + 1
            e_codes = flow.tile([P, NH, passes * P], U32, align_bytes=64)
            e_scales = flow.tile([P, NH, passes * P], U8, align_bytes=64)
            tile_live[(b, t)]["e_codes"] = e_codes
            tile_live[(b, t)]["e_scales"] = e_scales
            nc.vector.quantize_mx(
                out=e_codes[:].rearrange("p h c -> p (h c)").bitcast(FP8X4),
                scales=e_scales[:].rearrange("p h c -> p (h c)"),
                in_=tile_live[(b, t)]["e_grouped"][:].rearrange("p h c -> p (h c)"),
            )

        def invert_sums(b, t):
            inverse = small.tile([P, NH], F32)
            nc.vector.reciprocal(inverse[:], tile_live[(b, t)]["row_sums"][:])
            tile_live[(b, t)]["inverse"] = inverse

        def weighted_values(b, t):
            passes = t // 4 + 1
            e_codes, e_scales = tile_live[(b, t)]["e_codes"], tile_live[(b, t)]["e_scales"]
            acc = psum.tile([P, NH, D], F32, tag="bank")
            for h in range(NH):
                for g in range(passes):
                    nc.tensor.matmul_mx(
                        out=acc[:, h, :],
                        lhsT=e_codes[:, h, g * P : (g + 1) * P].bitcast(FP8X4),
                        lhsT_scale=e_scales[:, h, g * P : (g + 1) * P],
                        rhs=ready[b]["v_codes"][:, g, h * D : (h + 1) * D].bitcast(FP8X4),
                        rhs_scale=ready[b]["v_scales"][:, g, h * D : (h + 1) * D],
                        start=(g == 0),
                        stop=(g == passes - 1),
                    )
            tile_live[(b, t)]["acc"] = acc

        def normalise_and_store(b, t):
            result = results.tile([P, NH, D], F32)
            nc.vector.tensor_tensor(
                out=result[:],
                in0=tile_live[(b, t)]["acc"][:],
                in1=tile_live[(b, t)]["inverse"][:].unsqueeze(2).to_broadcast([P, NH, D]),
                op=ALU.mult,
            )
            nc.sync.dma_start(out=out[b, t * P : (t + 1) * P, :], in_=result[:].rearrange("p h d -> p (h d)"))

        w_grouped = const.tile([P, NH * H], BF16, align_bytes=64)
        w_codes = const.tile([P, H], U32, align_bytes=64)
        w_scales = const.tile([P, H], U8, align_bytes=64)

        def turn_job(job):
            if job[0] == "w":
                return turn_words(w_raw[:].bitcast(F32), w_grouped[:].bitcast(F32), job[1])
            if job[0] == "hid":
                return turn_hidden(job[1], job[2])
            return turn_half(*job)

        waiting = []
        for index, job in enumerate([("k", 0, 0, 0), ("q", 0, 0, 0), ("k", 0, 0, 1), ("q", 0, 0, 1)]):
            made = turn_job(job)
            for dst, src in waiting:
                copy_out(index % 2 == 0, dst, src)
            waiting = [made]

        steps_of_batch = NT * NH
        turn_at, hidden_at, project_at, bias_at, quantise_at, mx_at = {}, {}, {}, {}, {}, {}

        def plan(table, s, what):
            table.setdefault(s, []).append(what)

        for s, job in ((0, ("w", 0)), (0, ("w", 1)), (3, ("hid", 0, 0)), (3, ("hid", 0, 1)), (4, ("hid", 0, 2)), (4, ("hid", 0, 3))):
            plan(turn_at, s, job)
        plan(hidden_at, 6, 0)
        for b in range(B - 1):
            first = b * steps_of_batch + (5 if b == 0 else 0)
            jobs = [("k", b, 1, 0), ("k", b, 1, 1), ("q", b, 1, 0), ("q", b, 1, 1)]
            jobs.extend([("hid", b + 1, pair) for pair in range(4)])
            jobs.extend([("k", b + 1, 0, 0), ("k", b + 1, 0, 1), ("q", b + 1, 0, 0), ("q", b + 1, 0, 1)])
            if b + 2 == B:
                jobs.extend([("k", b + 1, 1, 0), ("k", b + 1, 1, 1), ("q", b + 1, 1, 0), ("q", b + 1, 1, 1)])
            for i, job in enumerate(jobs):
                plan(turn_at, first + i, job)
            plan(hidden_at, first + 9, b + 1)

        pieces = [(b, g, h) for b in range(B) for g in range(2) for h in range(NH)]
        for i, piece in enumerate(pieces[:NH]):
            plan(project_at, 7, piece)
            plan(bias_at, 8 + i // 2, piece)
        plan(quantise_at, 11, (0, 0))
        extra = [12] + [(B - 2) * steps_of_batch + j for j in (12, 16, 20, 24)]
        slots = sorted([s for s in range(10, n_units) if s % 4 == 2] + extra)
        for piece, s in zip(pieces[NH:], slots):
            plan(project_at, s, piece)
            plan(bias_at, s + (1 if s in extra else 2), piece)
            if piece[2] == NH - 1:
                plan(quantise_at, s + 4, (piece[0], piece[1]))

        for n in range(NH - 1, n_units, NH):
            plan(mx_at, max(n + 7, 2 * NH - 1 + 7), (units[n][0], units[n][1]))

        def completed(n):
            if 0 <= n < n_units and units[n][2] == NH - 1:
                return (units[n][0], units[n][1])
            return None

        for s in range(n_units + 9):
            b, j = s // steps_of_batch, s % steps_of_batch
            if 4 <= s < n_units + 4:
                turn(s - 4)
            if s < n_units:
                scores(s)
            for tile_done in mx_at.get(s, []):
                weighted_values(*tile_done)
            for piece in project_at.get(s, []):
                project_values(*piece)
            made = [turn_job(job) for job in turn_at.get(s, [])]
            if 1 <= s < n_units + 1:
                empty_scores(s - 1)
            for tile_done in mx_at.get(s - 1, []):
                normalise_and_store(*tile_done)
            for piece in bias_at.get(s, []):
                add_bias(*piece)
            if completed(s - 6) is not None:
                quantise(*completed(s - 6))
            if completed(s - 4) is not None:
                invert_sums(*completed(s - 4))
            for b_g in quantise_at.get(s, []):
                quantise_values(*b_g)
            if s == 2:
                nc.vector.quantize_mx(out=w_codes[:].bitcast(FP8X4), scales=w_scales[:], in_=w_grouped[:])
            for next_b in hidden_at.get(s, []):
                quantise_hidden(next_b)
            if 5 <= s < n_units + 5:
                regroup(s - 5)
            if 2 <= s < n_units + 2:
                exponentials(s - 2)
            for index, (dst, src) in enumerate(waiting):
                copy_out(index == 1, dst, src)
            waiting = made
            if s < n_units and b + 2 < B:
                if j == 13:
                    load_hidden(b + 2)
                if j in (15, 17, 19, 21):
                    load_half("kq"[(j - 15) // 2 % 2], (k, q)[(j - 15) // 2 % 2], b + 2, (j - 15) // 4)
